import numpy as np
import ml_dtypes


def mxq(x, axis, fmt="e4m3"):
    dtype, down = {"e4m3": (ml_dtypes.float8_e4m3fn, 7), "e5m2": (ml_dtypes.float8_e5m2, 14)}[fmt]
    v = np.moveaxis(np.asarray(x, np.float32).astype(ml_dtypes.bfloat16).astype(np.float64), axis, -1)
    blocks = v.reshape(v.shape[:-1] + (-1, 32))
    amax = np.abs(blocks).max(-1, keepdims=True)
    byte = np.maximum(np.where(amax > 0, np.frexp(amax)[1] - 1 + 127, 0) - down, 1)
    scale = np.exp2(byte - 127.0)
    codes = (blocks / scale).astype(np.float32).astype(dtype).astype(np.float64)
    return np.moveaxis((codes * scale).reshape(v.shape), -1, axis)


WIDE = False


def mx_kscale(k):
    if not WIDE:
        return np.ones(k)
    levels = np.array([10, -10, 5, -5, 0])
    a = np.random.permutation(np.resize(levels, k // 512 * 4)).reshape(k // 512, 4)
    idx = np.arange(k)
    return np.exp2(a[idx // 512, idx % 128 // 32])


BF16 = ml_dtypes.bfloat16


def bf(x):
    return np.asarray(x, np.float32).astype(BF16)


def f64(x):
    return np.asarray(x).astype(np.float64)


B, S, E, H, D = 2, 128, 8192, 4, 128


def setup_inputs():
    s = mx_kscale(E)
    ckv = 0.75 * D ** 0.25 / np.sqrt(E)
    cq = 3.0 / np.sqrt(E)
    return {"x": bf(np.random.standard_normal((B, S, E)) * s),
            "Wq": bf(np.random.standard_normal((E, H * D)) * cq / s[:, None]),
            "bq": bf(np.random.standard_normal(H * D) * 0.25),
            "Wk": bf(np.random.standard_normal((E, H * D)) * ckv / s[:, None]),
            "bk": bf(np.random.standard_normal(H * D)),
            "Wv": bf(np.random.standard_normal((E, H * D)) * ckv / s[:, None]),
            "bv": bf(np.random.standard_normal(H * D))}


def reference(x, Wq, bq, Wk, bk, Wv, bv):
    xq = mxq(f64(x), 2, "e4m3")

    def proj(W, bias):
        y = (xq @ mxq(f64(W), 0, "e4m3")) + f64(bias)
        return y.reshape(B, S, H, D).transpose(0, 2, 1, 3)

    q = proj(Wq, bq)
    k = proj(Wk, bk)
    v = proj(Wv, bv)
    kv = k * np.swapaxes(v, -1, -2) * (1.0 / np.sqrt(D))
    e = np.exp(kv - kv.max(axis=2, keepdims=True))
    attn = e / e.sum(axis=2, keepdims=True)
    return np.sum(attn * q, axis=2)

@@ -1,0 +1,289 @@
+import math
+from contextlib import ExitStack
+
+import concourse.mybir as mybir
+from concourse.masks import make_identity
+
+F32 = mybir.dt.float32
+BF16 = mybir.dt.bfloat16
+U32 = mybir.dt.uint32
+U8 = mybir.dt.uint8
+FP8X4 = mybir.dt.float8_e4m3fn_x4
+ALU = mybir.AluOpType
+ACT = mybir.ActivationFunctionType
+AXIS_X = mybir.AxisListType.X
+
+B, S, E, H, D = 2, 128, 8192, 4, 128
+P = 128
+PACK = 4
+K_PASS = P * PACK
+PASSES = E // K_PASS
+N = H * D
+ROWS = B * S
+GROUPS = B * H
+
+W_PASSES = 2
+W_LOADS = PASSES // W_PASSES
+X_PASSES = 4
+X_LOADS = PASSES // X_PASSES
+W_LOADS_PER_X = X_PASSES // W_PASSES
+PREFETCH = 8
+RUN = 4
+
+FLOPS = 2 * ROWS * E * 3 * N
+
+
+def tile_multihead_attention_pa_k_kernel(tc, x, Wq, bq, Wk, bk, Wv, bv, out):
+    nc = tc.nc
+    with ExitStack() as stack:
+        const = stack.enter_context(tc.tile_pool(name="const", bufs=1))
+        x_in = stack.enter_context(tc.tile_pool(name="x_in", bufs=X_LOADS))
+        x_stage = stack.enter_context(tc.tile_pool(name="x_stage", bufs=2))
+        w_in = stack.enter_context(tc.tile_pool(name="w_in", bufs=PREFETCH))
+        w_stage = stack.enter_context(tc.tile_pool(name="w_stage", bufs=3))
+        w_mx = stack.enter_context(tc.tile_pool(name="w_mx", bufs=3))
+        psum = stack.enter_context(tc.psum_pool(name="psum", bufs=8))
+
+        def load_x(q):
+            x_raw = x_in.tile([P, B * X_PASSES * K_PASS], BF16, name="x_raw")
+            k_cols = slice(q * X_PASSES * K_PASS, (q + 1) * X_PASSES * K_PASS)
+            nc.sync.dma_start(
+                out=x_raw[:].rearrange("s (b k) -> s b k", b=B),
+                in_=x[:, :, k_cols].rearrange("b s k -> s b k"),
+            )
+            return x_raw
+
+        def load_w(w, g):
+            w_raw = w_in.tile([P, W_PASSES * PACK * N], BF16, name="w_raw")
+            k_rows = slice(g * W_PASSES * K_PASS, (g + 1) * W_PASSES * K_PASS)
+            nc.sync.dma_start(
+                out=w_raw[:].rearrange("p (c r) -> p c r", c=W_PASSES),
+                in_=w[k_rows, :].rearrange("(c p t) n -> p c (t n)", c=W_PASSES, t=PACK),
+            )
+            return w_raw
+
+        stream = (
+            [("v", Wv, g) for g in range(W_LOADS)]
+            + [("k", Wk, g) for g in range(W_LOADS)]
+            + [("q", Wq, g) for g in range(W_LOADS)]
+        )
+        x_raws = {}
+        w_raws = {}
+
+        def load(i):
+            kind, w, g = stream[i]
+            if kind == "v" and g % W_LOADS_PER_X == 0:
+                x_raws[g // W_LOADS_PER_X] = load_x(g // W_LOADS_PER_X)
+            w_raws[i] = load_w(w, g)
+
+        for i in range(PREFETCH):
+            load(i)
+
+        ident_f32 = const.tile([P, P], F32)
+        make_identity(nc, ident_f32[:])
+        ident_bf16 = const.tile([P, P], BF16)
+        make_identity(nc, ident_bf16[:])
+
+        zero_col = const.tile([P, 1], F32)
+        nc.vector.memset(zero_col[:], 0.0)
+        one_col = const.tile([P, 1], F32)
+        nc.scalar.activation(out=one_col[:], in_=zero_col[:], func=ACT.Exp)
+
+        bias_rows = const.tile([P, D], BF16)
+        nc.vector.memset(bias_rows[:], 0.0)
+        nc.scalar.dma_start(out=bias_rows[0:H, :], in_=bk.rearrange("(h j) -> h j", h=H))
+        nc.scalar.dma_start(out=bias_rows[H : 2 * H, :], in_=bq.rearrange("(h j) -> h j", h=H))
+        bias_t = psum.tile([P, P], BF16, tag="bank")
+        nc.tensor.transpose(bias_t[:], bias_rows[:], ident_bf16[:])
+        bias_cols = const.tile([P, 2 * H], F32)
+        nc.vector.tensor_copy(out=bias_cols[:], in_=bias_t[:, 0 : 2 * H])
+        bk_cols = bias_cols[:, 0:H]
+        bq_cols = bias_cols[:, H : 2 * H]
+
+        bv_row = const.tile([P, N], BF16)
+        nc.vector.memset(bv_row[:], 0.0)
+        nc.scalar.dma_start(out=bv_row[0:1, :], in_=bv.rearrange("(o n) -> o n", o=1))
+        ones = const.tile([P, P], BF16)
+        nc.vector.memset(ones[:], 1.0)
+        bv_bank = psum.tile([P, N], F32, tag="bank")
+        nc.tensor.matmul(out=bv_bank[:], lhsT=ones[:], rhs=bv_row[:], start=True, stop=True)
+        bv_all = const.tile([P, N], F32)
+        nc.vector.tensor_copy(out=bv_all[:], in_=bv_bank[:])
+
+        result = const.tile([P, P], F32)
+        nc.vector.memset(result[:], 0.0)
+
+        x_codes = const.tile([P, PASSES * ROWS], U32, align_bytes=64)
+        x_scales = const.tile([P, PASSES * ROWS], U8, align_bytes=64)
+
+        def quantise_x(q, x_raw):
+            words = x_raw[:].bitcast(F32).rearrange(
+                "s (b c p u) -> s b c u p", b=B, c=X_PASSES, u=2
+            )
+            x_grouped = x_stage.tile([P, X_PASSES * ROWS * PACK], BF16, align_bytes=64)
+            grouped_words = x_grouped[:].bitcast(F32).rearrange(
+                "p (c m u) -> p c m u", c=X_PASSES, u=2
+            )
+            for c in range(X_PASSES):
+                x_t = psum.tile([P, 2 * ROWS], F32, tag="bank")
+                for u in range(2):
+                    for b in range(B):
+                        nc.tensor.transpose(
+                            x_t[:, u * ROWS + b * S : u * ROWS + (b + 1) * S],
+                            words[:, b, c, u, :],
+                            ident_f32[:],
+                        )
+                nc.scalar.copy(
+                    out=grouped_words[:, c], in_=x_t[:].rearrange("p (u m) -> p m u", u=2)
+                )
+            cols = slice(q * X_PASSES * ROWS, (q + 1) * X_PASSES * ROWS)
+            nc.vector.quantize_mx(
+                out=x_codes[:, cols].bitcast(FP8X4), scales=x_scales[:, cols], in_=x_grouped[:]
+            )
+
+        def quantise_w(w_raw):
+            w_grouped = w_stage.tile([P, W_PASSES * N * PACK], BF16, align_bytes=64)
+            half = N * PACK
+            nc.vector.tensor_copy(
+                out=w_grouped[:, 0:half].rearrange("p (n i t) -> p n t i", i=RUN, t=PACK),
+                in_=w_raw[:, 0:half].rearrange("p (t n i) -> p n t i", t=PACK, i=RUN),
+            )
+            nc.scalar.copy(
+                out=w_grouped[:, half : 2 * half].rearrange("p (n i t) -> p n t i", i=RUN, t=PACK),
+                in_=w_raw[:, half : 2 * half].rearrange("p (t n i) -> p n t i", t=PACK, i=RUN),
+            )
+            w_codes = w_mx.tile([P, W_PASSES * N], U32, align_bytes=64)
+            w_scales = w_mx.tile([P, W_PASSES * N], U8, align_bytes=64)
+            nc.vector.quantize_mx(
+                out=w_codes[:].bitcast(FP8X4), scales=w_scales[:], in_=w_grouped[:]
+            )
+            return w_codes, w_scales
+
+        def project(kind, g, banks, w_codes, w_scales):
+            for c in range(W_PASSES):
+                k_pass = g * W_PASSES + c
+                first = k_pass == 0
+                last = k_pass == PASSES - 1
+                if kind == "v":
+                    w_cols = slice(c * N, (c + 1) * N)
+                    for b in range(B):
+                        x_cols = slice(k_pass * ROWS + b * S, k_pass * ROWS + (b + 1) * S)
+                        nc.tensor.matmul_mx(
+                            out=banks[b][:],
+                            lhsT=x_codes[:, x_cols].bitcast(FP8X4),
+                            lhsT_scale=x_scales[:, x_cols],
+                            rhs=w_codes[:, w_cols].bitcast(FP8X4),
+                            rhs_scale=w_scales[:, w_cols],
+                            start=first,
+                            stop=last,
+                        )
+                else:
+                    x_cols = slice(k_pass * ROWS, (k_pass + 1) * ROWS)
+                    for h in range(H):
+                        w_cols = slice(c * N + h * D, c * N + (h + 1) * D)
+                        nc.tensor.matmul_mx(
+                            out=banks[h][:],
+                            lhsT=w_codes[:, w_cols].bitcast(FP8X4),
+                            lhsT_scale=w_scales[:, w_cols],
+                            rhs=x_codes[:, x_cols].bitcast(FP8X4),
+                            rhs_scale=x_scales[:, x_cols],
+                            start=first,
+                            stop=last,
+                        )
+
+        def by_head(t):
+            return t[:].rearrange("p (b h i) -> p h b i", b=B, h=H)
+
+        def by_group(t):
+            return t[:].rearrange("p (g i) -> p g i", g=GROUPS)
+
+        v_sb = const.tile([P, GROUPS * S], F32)
+        score = const.tile([P, GROUPS * S], F32)
+        expo = const.tile([P, GROUPS * S], F32)
+        weighted = const.tile([P, GROUPS * S], F32)
+        score_max = const.tile([P, GROUPS], F32)
+        exp_bias = const.tile([P, GROUPS], F32)
+        exp_sum = const.tile([P, GROUPS], F32)
+        inv_sum = const.tile([P, GROUPS], F32)
+        weighted_sum = const.tile([P, GROUPS], F32)
+        mean = const.tile([P, GROUPS], F32)
+        inv_sqrt_d = 1.0 / math.sqrt(D)
+
+        def after_v(banks):
+            for b in range(B):
+                nc.vector.tensor_tensor(
+                    out=v_sb[:, b * N : (b + 1) * N], in0=banks[b][:], in1=bv_all[:], op=ALU.add
+                )
+
+        def after_k(banks):
+            for h in range(H):
+                nc.vector.scalar_tensor_tensor(
+                    out=by_head(score)[:, h],
+                    in0=banks[h][:].rearrange("p (b i) -> p b i", b=B),
+                    scalar=bk_cols[:, h : h + 1],
+                    in1=by_head(v_sb)[:, h],
+                    op0=ALU.add,
+                    op1=ALU.mult,
+                )
+            nc.vector.tensor_reduce(
+                out=score_max[:], in_=by_group(score), axis=AXIS_X, op=ALU.max
+            )
+            nc.vector.tensor_scalar_mul(out=exp_bias[:], in0=score_max[:], scalar1=-inv_sqrt_d)
+            for g in range(GROUPS):
+                nc.scalar.activation(
+                    out=by_group(expo)[:, g],
+                    in_=by_group(score)[:, g],
+                    func=ACT.Exp,
+                    bias=exp_bias[:, g : g + 1],
+                    scale=inv_sqrt_d,
+                    accum_out=exp_sum[:, g : g + 1],
+                )
+            nc.vector.reciprocal(out=inv_sum[:], in_=exp_sum[:])
+
+        def after_q(banks):
+            for h in range(H):
+                nc.vector.tensor_tensor(
+                    out=by_head(weighted)[:, h],
+                    in0=banks[h][:].rearrange("p (b i) -> p b i", b=B),
+                    in1=by_head(expo)[:, h],
+                    op=ALU.mult,
+                )
+            nc.vector.tensor_reduce(
+                out=weighted_sum[:], in_=by_group(weighted), axis=AXIS_X, op=ALU.add
+            )
+            nc.vector.tensor_tensor(
+                out=mean[:], in0=weighted_sum[:], in1=inv_sum[:], op=ALU.mult
+            )
+            nc.vector.tensor_tensor(
+                out=result[:, 0:GROUPS].rearrange("p (b h) -> p b h", b=B),
+                in0=mean[:].rearrange("p (b h) -> p b h", b=B),
+                in1=bq_cols.unsqueeze(1).to_broadcast([P, B, H]),
+                op=ALU.add,
+            )
+            result_t = psum.tile([P, P], F32, tag="bank")
+            nc.tensor.transpose(result_t[:], result[:], ident_f32[:])
+            out_rows = const.tile([P, D], F32)
+            nc.vector.tensor_copy(out=out_rows[0:GROUPS, :], in_=result_t[0:GROUPS, :])
+            nc.sync.dma_start(out=out.rearrange("b h j -> (b h) j"), in_=out_rows[0:GROUPS, :])
+
+        banks = []
+        for i in range(len(stream)):
+            kind, w, g = stream[i]
+            if kind == "v" and g % W_LOADS_PER_X == 0:
+                quantise_x(g // W_LOADS_PER_X, x_raws[g // W_LOADS_PER_X])
+            w_codes, w_scales = quantise_w(w_raws[i])
+            if i + PREFETCH < len(stream):
+                load(i + PREFETCH)
+            if g == 0:
+                if kind == "v":
+                    banks = [psum.tile([P, N], F32, tag="bank", name="v_bank%d" % b) for b in range(B)]
+                else:
+                    banks = [psum.tile([P, ROWS], F32, tag="bank", name="%s_bank%d" % (kind, h)) for h in range(H)]
+            project(kind, g, banks, w_codes, w_scales)
+            if g == W_LOADS - 1:
+                if kind == "v":
+                    after_v(banks)
+                elif kind == "k":
+                    after_k(banks)
+                else:
+                    after_q(banks)

@@ -22,13 +22,12 @@ N = H * D
 ROWS = B * S
 GROUPS = B * H
 
-W_PASSES = 2
-W_LOADS = PASSES // W_PASSES
 X_PASSES = 4
 X_LOADS = PASSES // X_PASSES
-W_LOADS_PER_X = X_PASSES // W_PASSES
-PREFETCH = 8
+PREFETCH = 12
 RUN = 4
+VECTOR_COLS = N // 2
+EXP_LAG = 3
 
 FLOPS = 2 * ROWS * E * 3 * N
 
@@ -36,87 +35,82 @@ FLOPS = 2 * ROWS * E * 3 * N
 def tile_multihead_attention_pa_k_kernel(tc, x, Wq, bq, Wk, bk, Wv, bv, out):
     nc = tc.nc
     with ExitStack() as stack:
+        stack.enter_context(tc.manual_schedule())
         const = stack.enter_context(tc.tile_pool(name="const", bufs=1))
         x_in = stack.enter_context(tc.tile_pool(name="x_in", bufs=X_LOADS))
         x_stage = stack.enter_context(tc.tile_pool(name="x_stage", bufs=2))
         w_in = stack.enter_context(tc.tile_pool(name="w_in", bufs=PREFETCH))
-        w_stage = stack.enter_context(tc.tile_pool(name="w_stage", bufs=3))
-        w_mx = stack.enter_context(tc.tile_pool(name="w_mx", bufs=3))
+        w_stage = stack.enter_context(tc.tile_pool(name="w_stage", bufs=4))
+        w_mx = stack.enter_context(tc.tile_pool(name="w_mx", bufs=6))
         psum = stack.enter_context(tc.psum_pool(name="psum", bufs=8))
 
-        def load_x(q):
-            x_raw = x_in.tile([P, B * X_PASSES * K_PASS], BF16, name="x_raw")
-            k_cols = slice(q * X_PASSES * K_PASS, (q + 1) * X_PASSES * K_PASS)
-            nc.sync.dma_start(
-                out=x_raw[:].rearrange("s (b k) -> s b k", b=B),
-                in_=x[:, :, k_cols].rearrange("b s k -> s b k"),
-            )
-            return x_raw
-
-        def load_w(w, g):
-            w_raw = w_in.tile([P, W_PASSES * PACK * N], BF16, name="w_raw")
-            k_rows = slice(g * W_PASSES * K_PASS, (g + 1) * W_PASSES * K_PASS)
-            nc.sync.dma_start(
-                out=w_raw[:].rearrange("p (c r) -> p c r", c=W_PASSES),
-                in_=w[k_rows, :].rearrange("(c p t) n -> p c (t n)", c=W_PASSES, t=PACK),
-            )
-            return w_raw
-
-        stream = (
-            [("v", Wv, g) for g in range(W_LOADS)]
-            + [("k", Wk, g) for g in range(W_LOADS)]
-            + [("q", Wq, g) for g in range(W_LOADS)]
-        )
-        x_raws = {}
-        w_raws = {}
-
-        def load(i):
-            kind, w, g = stream[i]
-            if kind == "v" and g % W_LOADS_PER_X == 0:
-                x_raws[g // W_LOADS_PER_X] = load_x(g // W_LOADS_PER_X)
-            w_raws[i] = load_w(w, g)
-
-        for i in range(PREFETCH):
-            load(i)
-
+        bias_rows = const.tile([P, D], BF16)
+        nc.vector.memset(bias_rows[:], 0.0)
+        nc.scalar.dma_start(out=bias_rows[0:H, :], in_=bk.rearrange("(h j) -> h j", h=H))
+        nc.scalar.dma_start(out=bias_rows[H : 2 * H, :], in_=bq.rearrange("(h j) -> h j", h=H))
+        bv_row = const.tile([P, N], BF16)
+        nc.vector.memset(bv_row[:], 0.0)
+        nc.scalar.dma_start(out=bv_row[0:1, :], in_=bv.rearrange("(o n) -> o n", o=1))
+        ones = const.tile([P, P], BF16)
+        nc.vector.memset(ones[:], 1.0)
         ident_f32 = const.tile([P, P], F32)
         make_identity(nc, ident_f32[:])
         ident_bf16 = const.tile([P, P], BF16)
         make_identity(nc, ident_bf16[:])
+        bias_cols = const.tile([P, 2 * H], F32)
+        bk_cols = bias_cols[:, 0:H]
+        bq_cols = bias_cols[:, H : 2 * H]
+        bv_all = const.tile([P, N], F32)
+
+        def spread_biases():
+            bias_t = psum.tile([P, P], BF16, tag="bank")
+            nc.tensor.transpose(bias_t[:], bias_rows[:], ident_bf16[:])
+            nc.vector.tensor_copy(out=bias_cols[:], in_=bias_t[:, 0 : 2 * H])
+            bv_bank = psum.tile([P, N], F32, tag="bank")
+            nc.tensor.matmul(out=bv_bank[:], lhsT=ones[:], rhs=bv_row[:], start=True, stop=True)
+            nc.vector.tensor_copy(out=bv_all[:], in_=bv_bank[:])
 
         zero_col = const.tile([P, 1], F32)
         nc.vector.memset(zero_col[:], 0.0)
         one_col = const.tile([P, 1], F32)
         nc.scalar.activation(out=one_col[:], in_=zero_col[:], func=ACT.Exp)
 
-        bias_rows = const.tile([P, D], BF16)
-        nc.vector.memset(bias_rows[:], 0.0)
-        nc.scalar.dma_start(out=bias_rows[0:H, :], in_=bk.rearrange("(h j) -> h j", h=H))
-        nc.scalar.dma_start(out=bias_rows[H : 2 * H, :], in_=bq.rearrange("(h j) -> h j", h=H))
-        bias_t = psum.tile([P, P], BF16, tag="bank")
-        nc.tensor.transpose(bias_t[:], bias_rows[:], ident_bf16[:])
-        bias_cols = const.tile([P, 2 * H], F32)
-        nc.vector.tensor_copy(out=bias_cols[:], in_=bias_t[:, 0 : 2 * H])
-        bk_cols = bias_cols[:, 0:H]
-        bq_cols = bias_cols[:, H : 2 * H]
-
-        bv_row = const.tile([P, N], BF16)
-        nc.vector.memset(bv_row[:], 0.0)
-        nc.scalar.dma_start(out=bv_row[0:1, :], in_=bv.rearrange("(o n) -> o n", o=1))
-        ones = const.tile([P, P], BF16)
-        nc.vector.memset(ones[:], 1.0)
-        bv_bank = psum.tile([P, N], F32, tag="bank")
-        nc.tensor.matmul(out=bv_bank[:], lhsT=ones[:], rhs=bv_row[:], start=True, stop=True)
-        bv_all = const.tile([P, N], F32)
-        nc.vector.tensor_copy(out=bv_all[:], in_=bv_bank[:])
-
         result = const.tile([P, P], F32)
         nc.vector.memset(result[:], 0.0)
+
+        stream = (
+            [("v", Wv, c) for c in range(PASSES)]
+            + [("k", Wk, c) for c in range(PASSES)]
+            + [("q", Wq, c) for c in range(PASSES)]
+        )
+        x_raws = {}
+        w_raws = {}
+
+        def load(i):
+            kind, w, c = stream[i]
+            w_raw = w_in.tile([P, PACK * N], BF16, name="w_raw")
+            nc.sync.dma_start(
+                out=w_raw[:],
+                in_=w[c * K_PASS : (c + 1) * K_PASS, :].rearrange("(p t) n -> p (t n)", t=PACK),
+            )
+            w_raws[i] = w_raw
+            if kind == "v" and c % X_PASSES == 0:
+                q = c // X_PASSES
+                x_raw = x_in.tile([P, B * X_PASSES * K_PASS], BF16, name="x_raw")
+                k_cols = slice(q * X_PASSES * K_PASS, (q + 1) * X_PASSES * K_PASS)
+                nc.sync.dma_start(
+                    out=x_raw[:].rearrange("s (b k) -> s b k", b=B),
+                    in_=x[:, :, k_cols].rearrange("b s k -> s b k"),
+                )
+                x_raws[q] = x_raw
+
+        for i in range(PREFETCH):
+            load(i)
 
         x_codes = const.tile([P, PASSES * ROWS], U32, align_bytes=64)
         x_scales = const.tile([P, PASSES * ROWS], U8, align_bytes=64)
 
-        def quantise_x(q, x_raw):
+        def transpose_x(x_raw):
             words = x_raw[:].bitcast(F32).rearrange(
                 "s (b c p u) -> s b c u p", b=B, c=X_PASSES, u=2
             )
@@ -136,60 +130,68 @@ def tile_multihead_attention_pa_k_kernel(tc, x, Wq, bq, Wk, bk, Wv, bv, out):
                 nc.scalar.copy(
                     out=grouped_words[:, c], in_=x_t[:].rearrange("p (u m) -> p m u", u=2)
                 )
+            return x_grouped
+
+        def quantise_x(q, x_grouped):
             cols = slice(q * X_PASSES * ROWS, (q + 1) * X_PASSES * ROWS)
             nc.vector.quantize_mx(
                 out=x_codes[:, cols].bitcast(FP8X4), scales=x_scales[:, cols], in_=x_grouped[:]
             )
 
-        def quantise_w(w_raw):
-            w_grouped = w_stage.tile([P, W_PASSES * N * PACK], BF16, align_bytes=64)
-            half = N * PACK
-            nc.vector.tensor_copy(
-                out=w_grouped[:, 0:half].rearrange("p (n i t) -> p n t i", i=RUN, t=PACK),
-                in_=w_raw[:, 0:half].rearrange("p (t n i) -> p n t i", t=PACK, i=RUN),
-            )
-            nc.scalar.copy(
-                out=w_grouped[:, half : 2 * half].rearrange("p (n i t) -> p n t i", i=RUN, t=PACK),
-                in_=w_raw[:, half : 2 * half].rearrange("p (t n i) -> p n t i", t=PACK, i=RUN),
-            )
-            w_codes = w_mx.tile([P, W_PASSES * N], U32, align_bytes=64)
-            w_scales = w_mx.tile([P, W_PASSES * N], U8, align_bytes=64)
+        def regroup_w(w_raw):
+            w_grouped = w_stage.tile([P, N * PACK], BF16, align_bytes=64)
+            source = w_raw[:].rearrange("p (t r i) -> p r t i", t=PACK, i=RUN)
+            target = w_grouped[:].rearrange("p (r i t) -> p r t i", i=RUN, t=PACK)
+            split = VECTOR_COLS // RUN
+            nc.vector.tensor_copy(out=target[:, 0:split], in_=source[:, 0:split])
+            nc.scalar.copy(out=target[:, split:], in_=source[:, split:])
+            return w_grouped
+
+        def quantise_w(w_grouped):
+            w_codes = w_mx.tile([P, N], U32, align_bytes=64)
+            w_scales = w_mx.tile([P, N], U8, align_bytes=64)
             nc.vector.quantize_mx(
                 out=w_codes[:].bitcast(FP8X4), scales=w_scales[:], in_=w_grouped[:]
             )
             return w_codes, w_scales
 
-        def project(kind, g, banks, w_codes, w_scales):
-            for c in range(W_PASSES):
-                k_pass = g * W_PASSES + c
-                first = k_pass == 0
-                last = k_pass == PASSES - 1
-                if kind == "v":
-                    w_cols = slice(c * N, (c + 1) * N)
-                    for b in range(B):
-                        x_cols = slice(k_pass * ROWS + b * S, k_pass * ROWS + (b + 1) * S)
-                        nc.tensor.matmul_mx(
-                            out=banks[b][:],
-                            lhsT=x_codes[:, x_cols].bitcast(FP8X4),
-                            lhsT_scale=x_scales[:, x_cols],
-                            rhs=w_codes[:, w_cols].bitcast(FP8X4),
-                            rhs_scale=w_scales[:, w_cols],
-                            start=first,
-                            stop=last,
-                        )
-                else:
-                    x_cols = slice(k_pass * ROWS, (k_pass + 1) * ROWS)
-                    for h in range(H):
-                        w_cols = slice(c * N + h * D, c * N + (h + 1) * D)
-                        nc.tensor.matmul_mx(
-                            out=banks[h][:],
-                            lhsT=w_codes[:, w_cols].bitcast(FP8X4),
-                            lhsT_scale=w_scales[:, w_cols],
-                            rhs=x_codes[:, x_cols].bitcast(FP8X4),
-                            rhs_scale=x_scales[:, x_cols],
-                            start=first,
-                            stop=last,
-                        )
+        banks = {}
+
+        def project(kind, c, w_codes, w_scales):
+            if c == 0 and kind == "v":
+                banks[kind] = [
+                    psum.tile([P, N], F32, tag="bank", name="v_bank%d" % b) for b in range(B)
+                ]
+            elif c == 0:
+                banks[kind] = [
+                    psum.tile([P, ROWS], F32, tag="bank", name="%s_bank%d" % (kind, h))
+                    for h in range(H)
+                ]
+            if kind == "v":
+                for b in range(B):
+                    x_cols = slice(c * ROWS + b * S, c * ROWS + (b + 1) * S)
+                    nc.tensor.matmul_mx(
+                        out=banks[kind][b][:],
+                        lhsT=x_codes[:, x_cols].bitcast(FP8X4),
+                        lhsT_scale=x_scales[:, x_cols],
+                        rhs=w_codes[:].bitcast(FP8X4),
+                        rhs_scale=w_scales[:],
+                        start=(c == 0),
+                        stop=(c == PASSES - 1),
+                    )
+            else:
+                x_cols = slice(c * ROWS, (c + 1) * ROWS)
+                for h in range(H):
+                    w_cols = slice(h * D, (h + 1) * D)
+                    nc.tensor.matmul_mx(
+                        out=banks[kind][h][:],
+                        lhsT=w_codes[:, w_cols].bitcast(FP8X4),
+                        lhsT_scale=w_scales[:, w_cols],
+                        rhs=x_codes[:, x_cols].bitcast(FP8X4),
+                        rhs_scale=x_scales[:, x_cols],
+                        start=(c == 0),
+                        stop=(c == PASSES - 1),
+                    )
 
         def by_head(t):
             return t[:].rearrange("p (b h i) -> p h b i", b=B, h=H)
@@ -206,20 +208,22 @@ def tile_multihead_attention_pa_k_kernel(tc, x, Wq, bq, Wk, bk, Wv, bv, out):
         exp_sum = const.tile([P, GROUPS], F32)
         inv_sum = const.tile([P, GROUPS], F32)
         weighted_sum = const.tile([P, GROUPS], F32)
-        mean = const.tile([P, GROUPS], F32)
         inv_sqrt_d = 1.0 / math.sqrt(D)
 
-        def after_v(banks):
+        def add_bv():
             for b in range(B):
                 nc.vector.tensor_tensor(
-                    out=v_sb[:, b * N : (b + 1) * N], in0=banks[b][:], in1=bv_all[:], op=ALU.add
+                    out=v_sb[:, b * N : (b + 1) * N],
+                    in0=banks["v"][b][:],
+                    in1=bv_all[:],
+                    op=ALU.add,
                 )
 
-        def after_k(banks):
+        def scores():
             for h in range(H):
                 nc.vector.scalar_tensor_tensor(
                     out=by_head(score)[:, h],
-                    in0=banks[h][:].rearrange("p (b i) -> p b i", b=B),
+                    in0=banks["k"][h][:].rearrange("p (b i) -> p b i", b=B),
                     scalar=bk_cols[:, h : h + 1],
                     in1=by_head(v_sb)[:, h],
                     op0=ALU.add,
@@ -229,6 +233,8 @@ def tile_multihead_attention_pa_k_kernel(tc, x, Wq, bq, Wk, bk, Wv, bv, out):
                 out=score_max[:], in_=by_group(score), axis=AXIS_X, op=ALU.max
             )
             nc.vector.tensor_scalar_mul(out=exp_bias[:], in0=score_max[:], scalar1=-inv_sqrt_d)
+
+        def exponentials():
             for g in range(GROUPS):
                 nc.scalar.activation(
                     out=by_group(expo)[:, g],
@@ -238,27 +244,23 @@ def tile_multihead_attention_pa_k_kernel(tc, x, Wq, bq, Wk, bk, Wv, bv, out):
                     scale=inv_sqrt_d,
                     accum_out=exp_sum[:, g : g + 1],
                 )
-            nc.vector.reciprocal(out=inv_sum[:], in_=exp_sum[:])
 
-        def after_q(banks):
+        def pool_q():
+            nc.vector.reciprocal(out=inv_sum[:], in_=exp_sum[:])
             for h in range(H):
-                nc.vector.tensor_tensor(
+                nc.vector.scalar_tensor_tensor(
                     out=by_head(weighted)[:, h],
-                    in0=banks[h][:].rearrange("p (b i) -> p b i", b=B),
+                    in0=banks["q"][h][:].rearrange("p (b i) -> p b i", b=B),
+                    scalar=bq_cols[:, h : h + 1],
                     in1=by_head(expo)[:, h],
-                    op=ALU.mult,
+                    op0=ALU.add,
+                    op1=ALU.mult,
                 )
             nc.vector.tensor_reduce(
                 out=weighted_sum[:], in_=by_group(weighted), axis=AXIS_X, op=ALU.add
             )
             nc.vector.tensor_tensor(
-                out=mean[:], in0=weighted_sum[:], in1=inv_sum[:], op=ALU.mult
-            )
-            nc.vector.tensor_tensor(
-                out=result[:, 0:GROUPS].rearrange("p (b h) -> p b h", b=B),
-                in0=mean[:].rearrange("p (b h) -> p b h", b=B),
-                in1=bq_cols.unsqueeze(1).to_broadcast([P, B, H]),
-                op=ALU.add,
+                out=result[:, 0:GROUPS], in0=weighted_sum[:], in1=inv_sum[:], op=ALU.mult
             )
             result_t = psum.tile([P, P], F32, tag="bank")
             nc.tensor.transpose(result_t[:], result[:], ident_f32[:])
@@ -266,24 +268,30 @@ def tile_multihead_attention_pa_k_kernel(tc, x, Wq, bq, Wk, bk, Wv, bv, out):
             nc.vector.tensor_copy(out=out_rows[0:GROUPS, :], in_=result_t[0:GROUPS, :])
             nc.sync.dma_start(out=out.rearrange("b h j -> (b h) j"), in_=out_rows[0:GROUPS, :])
 
-        banks = []
-        for i in range(len(stream)):
-            kind, w, g = stream[i]
-            if kind == "v" and g % W_LOADS_PER_X == 0:
-                quantise_x(g // W_LOADS_PER_X, x_raws[g // W_LOADS_PER_X])
-            w_codes, w_scales = quantise_w(w_raws[i])
-            if i + PREFETCH < len(stream):
-                load(i + PREFETCH)
-            if g == 0:
-                if kind == "v":
-                    banks = [psum.tile([P, N], F32, tag="bank", name="v_bank%d" % b) for b in range(B)]
-                else:
-                    banks = [psum.tile([P, ROWS], F32, tag="bank", name="%s_bank%d" % (kind, h)) for h in range(H)]
-            project(kind, g, banks, w_codes, w_scales)
-            if g == W_LOADS - 1:
-                if kind == "v":
-                    after_v(banks)
-                elif kind == "k":
-                    after_k(banks)
-                else:
-                    after_q(banks)
+        v_done = PASSES
+        k_done = 2 * PASSES
+        w_grouped = {}
+        for i in range(len(stream) + 1):
+            if i == 1:
+                spread_biases()
+            if i < len(stream):
+                kind, w, c = stream[i]
+                new_x = kind == "v" and c % X_PASSES == 1
+                if new_x:
+                    x_grouped = transpose_x(x_raws[c // X_PASSES])
+                w_grouped[i] = regroup_w(w_raws[i])
+                if new_x:
+                    quantise_x(c // X_PASSES, x_grouped)
+                if i + PREFETCH < len(stream):
+                    load(i + PREFETCH)
+            if i >= 1:
+                kind, w, c = stream[i - 1]
+                w_codes, w_scales = quantise_w(w_grouped[i - 1])
+                project(kind, c, w_codes, w_scales)
+            if i == v_done + 1:
+                add_bv()
+            if i == k_done + 1:
+                scores()
+            if i == k_done + 1 + EXP_LAG:
+                exponentials()
+        pool_q()

@@ -26,7 +26,7 @@ X_PASSES = 4
 X_LOADS = PASSES // X_PASSES
 PREFETCH = 12
 RUN = 4
-VECTOR_COLS = N // 2
+VECTOR_COLS = 248
 EXP_LAG = 3
 
 FLOPS = 2 * ROWS * E * 3 * N
@@ -35,13 +35,12 @@ FLOPS = 2 * ROWS * E * 3 * N
 def tile_multihead_attention_pa_k_kernel(tc, x, Wq, bq, Wk, bk, Wv, bv, out):
     nc = tc.nc
     with ExitStack() as stack:
-        stack.enter_context(tc.manual_schedule())
         const = stack.enter_context(tc.tile_pool(name="const", bufs=1))
         x_in = stack.enter_context(tc.tile_pool(name="x_in", bufs=X_LOADS))
-        x_stage = stack.enter_context(tc.tile_pool(name="x_stage", bufs=2))
+        x_stage = stack.enter_context(tc.tile_pool(name="x_stage", bufs=3))
         w_in = stack.enter_context(tc.tile_pool(name="w_in", bufs=PREFETCH))
-        w_stage = stack.enter_context(tc.tile_pool(name="w_stage", bufs=4))
-        w_mx = stack.enter_context(tc.tile_pool(name="w_mx", bufs=6))
+        w_stage = stack.enter_context(tc.tile_pool(name="w_stage", bufs=6))
+        w_mx = stack.enter_context(tc.tile_pool(name="w_mx", bufs=8))
         psum = stack.enter_context(tc.psum_pool(name="psum", bufs=8))
 
         bias_rows = const.tile([P, D], BF16)
@@ -110,30 +109,30 @@ def tile_multihead_attention_pa_k_kernel(tc, x, Wq, bq, Wk, bk, Wv, bv, out):
         x_codes = const.tile([P, PASSES * ROWS], U32, align_bytes=64)
         x_scales = const.tile([P, PASSES * ROWS], U8, align_bytes=64)
 
-        def transpose_x(x_raw):
-            words = x_raw[:].bitcast(F32).rearrange(
+        def transpose_x(c):
+            words = x_raws[c // X_PASSES][:].bitcast(F32).rearrange(
                 "s (b c p u) -> s b c u p", b=B, c=X_PASSES, u=2
             )
-            x_grouped = x_stage.tile([P, X_PASSES * ROWS * PACK], BF16, align_bytes=64)
-            grouped_words = x_grouped[:].bitcast(F32).rearrange(
-                "p (c m u) -> p c m u", c=X_PASSES, u=2
+            x_t = psum.tile([P, 2 * ROWS], F32, tag="bank")
+            for u in range(2):
+                for b in range(B):
+                    nc.tensor.transpose(
+                        x_t[:, u * ROWS + b * S : u * ROWS + (b + 1) * S],
+                        words[:, b, c % X_PASSES, u, :],
+                        ident_f32[:],
+                    )
+            return x_t
+
+        def regroup_x(x_t):
+            x_grouped = x_stage.tile([P, ROWS * PACK], BF16, align_bytes=64)
+            nc.scalar.copy(
+                out=x_grouped[:].bitcast(F32).rearrange("p (m u) -> p m u", u=2),
+                in_=x_t[:].rearrange("p (u m) -> p m u", u=2),
             )
-            for c in range(X_PASSES):
-                x_t = psum.tile([P, 2 * ROWS], F32, tag="bank")
-                for u in range(2):
-                    for b in range(B):
-                        nc.tensor.transpose(
-                            x_t[:, u * ROWS + b * S : u * ROWS + (b + 1) * S],
-                            words[:, b, c, u, :],
-                            ident_f32[:],
-                        )
-                nc.scalar.copy(
-                    out=grouped_words[:, c], in_=x_t[:].rearrange("p (u m) -> p m u", u=2)
-                )
             return x_grouped
 
-        def quantise_x(q, x_grouped):
-            cols = slice(q * X_PASSES * ROWS, (q + 1) * X_PASSES * ROWS)
+        def quantise_x(c, x_grouped):
+            cols = slice(c * ROWS, (c + 1) * ROWS)
             nc.vector.quantize_mx(
                 out=x_codes[:, cols].bitcast(FP8X4), scales=x_scales[:, cols], in_=x_grouped[:]
             )
@@ -270,23 +269,25 @@ def tile_multihead_attention_pa_k_kernel(tc, x, Wq, bq, Wk, bk, Wv, bv, out):
 
         v_done = PASSES
         k_done = 2 * PASSES
-        w_grouped = {}
+        w_ready = {}
+        x_ready = {}
         for i in range(len(stream) + 1):
             if i == 1:
                 spread_biases()
             if i < len(stream):
                 kind, w, c = stream[i]
-                new_x = kind == "v" and c % X_PASSES == 1
-                if new_x:
-                    x_grouped = transpose_x(x_raws[c // X_PASSES])
-                w_grouped[i] = regroup_w(w_raws[i])
-                if new_x:
-                    quantise_x(c // X_PASSES, x_grouped)
+                if kind == "v":
+                    x_t = transpose_x(c)
+                w_ready[i] = regroup_w(w_raws[i])
+                if kind == "v":
+                    x_ready[c] = regroup_x(x_t)
                 if i + PREFETCH < len(stream):
                     load(i + PREFETCH)
             if i >= 1:
                 kind, w, c = stream[i - 1]
-                w_codes, w_scales = quantise_w(w_grouped[i - 1])
+                if kind == "v":
+                    quantise_x(c, x_ready[c])
+                w_codes, w_scales = quantise_w(w_ready[i - 1])
                 project(kind, c, w_codes, w_scales)
             if i == v_done + 1:
                 add_bv()

@@ -22,11 +22,12 @@ N = H * D
 ROWS = B * S
 GROUPS = B * H
 
-X_PASSES = 4
+X_PASSES = 2
 X_LOADS = PASSES // X_PASSES
 PREFETCH = 12
 RUN = 4
 VECTOR_COLS = 248
+X_LAG = 2
 EXP_LAG = 3
 
 FLOPS = 2 * ROWS * E * 3 * N
@@ -93,7 +94,7 @@ def tile_multihead_attention_pa_k_kernel(tc, x, Wq, bq, Wk, bk, Wv, bv, out):
                 in_=w[c * K_PASS : (c + 1) * K_PASS, :].rearrange("(p t) n -> p (t n)", t=PACK),
             )
             w_raws[i] = w_raw
-            if kind == "v" and c % X_PASSES == 0:
+            if kind == "v" and c % X_PASSES == X_PASSES - 1:
                 q = c // X_PASSES
                 x_raw = x_in.tile([P, B * X_PASSES * K_PASS], BF16, name="x_raw")
                 k_cols = slice(q * X_PASSES * K_PASS, (q + 1) * X_PASSES * K_PASS)
@@ -267,27 +268,32 @@ def tile_multihead_attention_pa_k_kernel(tc, x, Wq, bq, Wk, bk, Wv, bv, out):
             nc.vector.tensor_copy(out=out_rows[0:GROUPS, :], in_=result_t[0:GROUPS, :])
             nc.sync.dma_start(out=out.rearrange("b h j -> (b h) j"), in_=out_rows[0:GROUPS, :])
 
-        v_done = PASSES
+        v_done = PASSES + X_LAG
         k_done = 2 * PASSES
         w_ready = {}
         x_ready = {}
+        v_ready = {}
         for i in range(len(stream) + 1):
             if i == 1:
                 spread_biases()
+            x_c = i - X_LAG
+            if 0 <= x_c < PASSES:
+                x_t = transpose_x(x_c)
             if i < len(stream):
-                kind, w, c = stream[i]
-                if kind == "v":
-                    x_t = transpose_x(c)
                 w_ready[i] = regroup_w(w_raws[i])
-                if kind == "v":
-                    x_ready[c] = regroup_x(x_t)
                 if i + PREFETCH < len(stream):
                     load(i + PREFETCH)
+            if 0 <= x_c < PASSES:
+                x_ready[x_c] = regroup_x(x_t)
             if i >= 1:
                 kind, w, c = stream[i - 1]
-                if kind == "v":
-                    quantise_x(c, x_ready[c])
                 w_codes, w_scales = quantise_w(w_ready[i - 1])
+                if kind == "v":
+                    v_ready[c] = (w_codes, w_scales)
+            if 0 <= x_c - 1 < PASSES:
+                quantise_x(x_c - 1, x_ready[x_c - 1])
+                project("v", x_c - 1, *v_ready[x_c - 1])
+            if i >= 1 and kind != "v":
                 project(kind, c, w_codes, w_scales)
             if i == v_done + 1:
                 add_bv()

@@ -25,7 +25,7 @@ GROUPS = B * H
 X_PASSES = 2
 X_LOADS = PASSES // X_PASSES
 PREFETCH = 12
-RUN = 4
+RUN = 2
 VECTOR_COLS = 248
 X_LAG = 2
 EXP_LAG = 3

@@ -26,7 +26,7 @@ X_PASSES = 2
 X_LOADS = PASSES // X_PASSES
 PREFETCH = 12
 RUN = 2
-VECTOR_COLS = 248
+VECTOR_COLS = {"v": 280, "k": 236, "q": 236}
 X_LAG = 2
 EXP_LAG = 3
 
@@ -138,11 +138,11 @@ def tile_multihead_attention_pa_k_kernel(tc, x, Wq, bq, Wk, bk, Wv, bv, out):
                 out=x_codes[:, cols].bitcast(FP8X4), scales=x_scales[:, cols], in_=x_grouped[:]
             )
 
-        def regroup_w(w_raw):
+        def regroup_w(kind, w_raw):
             w_grouped = w_stage.tile([P, N * PACK], BF16, align_bytes=64)
             source = w_raw[:].rearrange("p (t r i) -> p r t i", t=PACK, i=RUN)
             target = w_grouped[:].rearrange("p (r i t) -> p r t i", i=RUN, t=PACK)
-            split = VECTOR_COLS // RUN
+            split = VECTOR_COLS[kind] // RUN
             nc.vector.tensor_copy(out=target[:, 0:split], in_=source[:, 0:split])
             nc.scalar.copy(out=target[:, split:], in_=source[:, split:])
             return w_grouped
@@ -280,7 +280,7 @@ def tile_multihead_attention_pa_k_kernel(tc, x, Wq, bq, Wk, bk, Wv, bv, out):
             if 0 <= x_c < PASSES:
                 x_t = transpose_x(x_c)
             if i < len(stream):
-                w_ready[i] = regroup_w(w_raws[i])
+                w_ready[i] = regroup_w(stream[i][0], w_raws[i])
                 if i + PREFETCH < len(stream):
                     load(i + PREFETCH)
             if 0 <= x_c < PASSES:

@@ -26,7 +26,9 @@ X_PASSES = 2
 X_LOADS = PASSES // X_PASSES
 PREFETCH = 12
 RUN = 2
-VECTOR_COLS = {"v": 280, "k": 236, "q": 236}
+VECTOR_COLS = {"v": 280, "k": 236, "q": 248}
+SCORE_ROUNDS = 5
+VECTOR_COLS_BESIDE_SCORES = 192
 X_LAG = 2
 EXP_LAG = 3
 
@@ -138,21 +140,27 @@ def tile_multihead_attention_pa_k_kernel(tc, x, Wq, bq, Wk, bk, Wv, bv, out):
                 out=x_codes[:, cols].bitcast(FP8X4), scales=x_scales[:, cols], in_=x_grouped[:]
             )
 
-        def regroup_w(kind, w_raw):
+        def regroup_w(kind, c, w_raw):
             w_grouped = w_stage.tile([P, N * PACK], BF16, align_bytes=64)
             source = w_raw[:].rearrange("p (t r i) -> p r t i", t=PACK, i=RUN)
             target = w_grouped[:].rearrange("p (r i t) -> p r t i", i=RUN, t=PACK)
-            split = VECTOR_COLS[kind] // RUN
+            beside_scores = kind == "q" and c < SCORE_ROUNDS
+            split = (VECTOR_COLS_BESIDE_SCORES if beside_scores else VECTOR_COLS[kind]) // RUN
             nc.vector.tensor_copy(out=target[:, 0:split], in_=source[:, 0:split])
             nc.scalar.copy(out=target[:, split:], in_=source[:, split:])
             return w_grouped
 
-        def quantise_w(w_grouped):
+        def quantise_w(w_grouped, pieces):
             w_codes = w_mx.tile([P, N], U32, align_bytes=64)
             w_scales = w_mx.tile([P, N], U8, align_bytes=64)
-            nc.vector.quantize_mx(
-                out=w_codes[:].bitcast(FP8X4), scales=w_scales[:], in_=w_grouped[:]
-            )
+            width = N // pieces
+            for n0 in range(0, N, width):
+                cols = slice(n0, n0 + width)
+                nc.vector.quantize_mx(
+                    out=w_codes[:, cols].bitcast(FP8X4),
+                    scales=w_scales[:, cols],
+                    in_=w_grouped[:, n0 * PACK : (n0 + width) * PACK],
+                )
             return w_codes, w_scales
 
         banks = {}
@@ -203,6 +211,7 @@ def tile_multihead_attention_pa_k_kernel(tc, x, Wq, bq, Wk, bk, Wv, bv, out):
         score = const.tile([P, GROUPS * S], F32)
         expo = const.tile([P, GROUPS * S], F32)
         weighted = const.tile([P, GROUPS * S], F32)
+        summed = const.tile([P, GROUPS * S], F32)
         score_max = const.tile([P, GROUPS], F32)
         exp_bias = const.tile([P, GROUPS], F32)
         exp_sum = const.tile([P, GROUPS], F32)
@@ -246,7 +255,6 @@ def tile_multihead_attention_pa_k_kernel(tc, x, Wq, bq, Wk, bk, Wv, bv, out):
                 )
 
         def pool_q():
-            nc.vector.reciprocal(out=inv_sum[:], in_=exp_sum[:])
             for h in range(H):
                 nc.vector.scalar_tensor_tensor(
                     out=by_head(weighted)[:, h],
@@ -256,8 +264,20 @@ def tile_multihead_attention_pa_k_kernel(tc, x, Wq, bq, Wk, bk, Wv, bv, out):
                     op0=ALU.add,
                     op1=ALU.mult,
                 )
+                if h < H - 1:
+                    for b in range(B):
+                        g = b * H + h
+                        nc.scalar.activation(
+                            out=by_group(summed)[:, g],
+                            in_=by_group(weighted)[:, g],
+                            func=ACT.Copy,
+                            accum_out=weighted_sum[:, g : g + 1],
+                        )
             nc.vector.tensor_reduce(
-                out=weighted_sum[:], in_=by_group(weighted), axis=AXIS_X, op=ALU.add
+                out=weighted_sum[:, H - 1 :: H],
+                in_=by_head(weighted)[:, H - 1],
+                axis=AXIS_X,
+                op=ALU.add,
             )
             nc.vector.tensor_tensor(
                 out=result[:, 0:GROUPS], in0=weighted_sum[:], in1=inv_sum[:], op=ALU.mult
@@ -271,23 +291,24 @@ def tile_multihead_attention_pa_k_kernel(tc, x, Wq, bq, Wk, bk, Wv, bv, out):
         v_done = PASSES + X_LAG
         k_done = 2 * PASSES
         w_ready = {}
+        x_banks = {}
         x_ready = {}
         v_ready = {}
         for i in range(len(stream) + 1):
             if i == 1:
                 spread_biases()
             x_c = i - X_LAG
-            if 0 <= x_c < PASSES:
-                x_t = transpose_x(x_c)
+            if 0 <= x_c + 1 < PASSES:
+                x_banks[x_c + 1] = transpose_x(x_c + 1)
             if i < len(stream):
-                w_ready[i] = regroup_w(stream[i][0], w_raws[i])
+                w_ready[i] = regroup_w(stream[i][0], stream[i][2], w_raws[i])
                 if i + PREFETCH < len(stream):
                     load(i + PREFETCH)
             if 0 <= x_c < PASSES:
-                x_ready[x_c] = regroup_x(x_t)
+                x_ready[x_c] = regroup_x(x_banks[x_c])
             if i >= 1:
                 kind, w, c = stream[i - 1]
-                w_codes, w_scales = quantise_w(w_ready[i - 1])
+                w_codes, w_scales = quantise_w(w_ready[i - 1], 2 if i == len(stream) else 1)
                 if kind == "v":
                     v_ready[c] = (w_codes, w_scales)
             if 0 <= x_c - 1 < PASSES:
@@ -301,4 +322,6 @@ def tile_multihead_attention_pa_k_kernel(tc, x, Wq, bq, Wk, bk, Wv, bv, out):
                 scores()
             if i == k_done + 1 + EXP_LAG:
                 exponentials()
+            if i == k_done + 1 + 2 * EXP_LAG:
+                nc.vector.reciprocal(out=inv_sum[:], in_=exp_sum[:])
         pool_q()

import math
from contextlib import ExitStack

import concourse.mybir as mybir
from concourse.masks import make_identity

F32 = mybir.dt.float32
BF16 = mybir.dt.bfloat16
U32 = mybir.dt.uint32
U8 = mybir.dt.uint8
FP8X4 = mybir.dt.float8_e4m3fn_x4
ALU = mybir.AluOpType
ACT = mybir.ActivationFunctionType
AXIS_X = mybir.AxisListType.X

B, S, E, H, D = 2, 128, 8192, 4, 128
P = 128
PACK = 4
K_PASS = P * PACK
PASSES = E // K_PASS
N = H * D
ROWS = B * S
GROUPS = B * H

X_PASSES = 2
X_LOADS = PASSES // X_PASSES
PREFETCH = 12
RUN = 2
VECTOR_COLS = {"v": 280, "k": 236, "q": 248}
SCORE_ROUNDS = 5
VECTOR_COLS_BESIDE_SCORES = 192
X_LAG = 2
EXP_LAG = 3

FLOPS = 2 * ROWS * E * 3 * N


def tile_multihead_attention_pa_k_kernel(tc, x, Wq, bq, Wk, bk, Wv, bv, out):
    nc = tc.nc
    with ExitStack() as stack:
        const = stack.enter_context(tc.tile_pool(name="const", bufs=1))
        x_in = stack.enter_context(tc.tile_pool(name="x_in", bufs=X_LOADS))
        x_stage = stack.enter_context(tc.tile_pool(name="x_stage", bufs=3))
        w_in = stack.enter_context(tc.tile_pool(name="w_in", bufs=PREFETCH))
        w_stage = stack.enter_context(tc.tile_pool(name="w_stage", bufs=6))
        w_mx = stack.enter_context(tc.tile_pool(name="w_mx", bufs=8))
        psum = stack.enter_context(tc.psum_pool(name="psum", bufs=8))

        bias_rows = const.tile([P, D], BF16)
        nc.vector.memset(bias_rows[:], 0.0)
        nc.scalar.dma_start(out=bias_rows[0:H, :], in_=bk.rearrange("(h j) -> h j", h=H))
        nc.scalar.dma_start(out=bias_rows[H : 2 * H, :], in_=bq.rearrange("(h j) -> h j", h=H))
        bv_row = const.tile([P, N], BF16)
        nc.vector.memset(bv_row[:], 0.0)
        nc.scalar.dma_start(out=bv_row[0:1, :], in_=bv.rearrange("(o n) -> o n", o=1))
        ones = const.tile([P, P], BF16)
        nc.vector.memset(ones[:], 1.0)
        ident_f32 = const.tile([P, P], F32)
        make_identity(nc, ident_f32[:])
        ident_bf16 = const.tile([P, P], BF16)
        make_identity(nc, ident_bf16[:])
        bias_cols = const.tile([P, 2 * H], F32)
        bk_cols = bias_cols[:, 0:H]
        bq_cols = bias_cols[:, H : 2 * H]
        bv_all = const.tile([P, N], F32)

        def spread_biases():
            bias_t = psum.tile([P, P], BF16, tag="bank")
            nc.tensor.transpose(bias_t[:], bias_rows[:], ident_bf16[:])
            nc.vector.tensor_copy(out=bias_cols[:], in_=bias_t[:, 0 : 2 * H])
            bv_bank = psum.tile([P, N], F32, tag="bank")
            nc.tensor.matmul(out=bv_bank[:], lhsT=ones[:], rhs=bv_row[:], start=True, stop=True)
            nc.vector.tensor_copy(out=bv_all[:], in_=bv_bank[:])

        zero_col = const.tile([P, 1], F32)
        nc.vector.memset(zero_col[:], 0.0)
        one_col = const.tile([P, 1], F32)
        nc.scalar.activation(out=one_col[:], in_=zero_col[:], func=ACT.Exp)

        result = const.tile([P, P], F32)
        nc.vector.memset(result[:], 0.0)

        stream = (
            [("v", Wv, c) for c in range(PASSES)]
            + [("k", Wk, c) for c in range(PASSES)]
            + [("q", Wq, c) for c in range(PASSES)]
        )
        x_raws = {}
        w_raws = {}

        def load(i):
            kind, w, c = stream[i]
            w_raw = w_in.tile([P, PACK * N], BF16, name="w_raw")
            nc.sync.dma_start(
                out=w_raw[:],
                in_=w[c * K_PASS : (c + 1) * K_PASS, :].rearrange("(p t) n -> p (t n)", t=PACK),
            )
            w_raws[i] = w_raw
            if kind == "v" and c % X_PASSES == X_PASSES - 1:
                q = c // X_PASSES
                x_raw = x_in.tile([P, B * X_PASSES * K_PASS], BF16, name="x_raw")
                k_cols = slice(q * X_PASSES * K_PASS, (q + 1) * X_PASSES * K_PASS)
                nc.sync.dma_start(
                    out=x_raw[:].rearrange("s (b k) -> s b k", b=B),
                    in_=x[:, :, k_cols].rearrange("b s k -> s b k"),
                )
                x_raws[q] = x_raw

        for i in range(PREFETCH):
            load(i)

        x_codes = const.tile([P, PASSES * ROWS], U32, align_bytes=64)
        x_scales = const.tile([P, PASSES * ROWS], U8, align_bytes=64)

        def transpose_x(c):
            words = x_raws[c // X_PASSES][:].bitcast(F32).rearrange(
                "s (b c p u) -> s b c u p", b=B, c=X_PASSES, u=2
            )
            x_t = psum.tile([P, 2 * ROWS], F32, tag="bank")
            for u in range(2):
                for b in range(B):
                    nc.tensor.transpose(
                        x_t[:, u * ROWS + b * S : u * ROWS + (b + 1) * S],
                        words[:, b, c % X_PASSES, u, :],
                        ident_f32[:],
                    )
            return x_t

        def regroup_x(x_t):
            x_grouped = x_stage.tile([P, ROWS * PACK], BF16, align_bytes=64)
            nc.scalar.copy(
                out=x_grouped[:].bitcast(F32).rearrange("p (m u) -> p m u", u=2),
                in_=x_t[:].rearrange("p (u m) -> p m u", u=2),
            )
            return x_grouped

        def quantise_x(c, x_grouped):
            cols = slice(c * ROWS, (c + 1) * ROWS)
            nc.vector.quantize_mx(
                out=x_codes[:, cols].bitcast(FP8X4), scales=x_scales[:, cols], in_=x_grouped[:]
            )

        def regroup_w(kind, c, w_raw):
            w_grouped = w_stage.tile([P, N * PACK], BF16, align_bytes=64)
            source = w_raw[:].rearrange("p (t r i) -> p r t i", t=PACK, i=RUN)
            target = w_grouped[:].rearrange("p (r i t) -> p r t i", i=RUN, t=PACK)
            beside_scores = kind == "q" and c < SCORE_ROUNDS
            split = (VECTOR_COLS_BESIDE_SCORES if beside_scores else VECTOR_COLS[kind]) // RUN
            nc.vector.tensor_copy(out=target[:, 0:split], in_=source[:, 0:split])
            nc.scalar.copy(out=target[:, split:], in_=source[:, split:])
            return w_grouped

        def quantise_w(w_grouped, pieces):
            w_codes = w_mx.tile([P, N], U32, align_bytes=64)
            w_scales = w_mx.tile([P, N], U8, align_bytes=64)
            width = N // pieces
            for n0 in range(0, N, width):
                cols = slice(n0, n0 + width)
                nc.vector.quantize_mx(
                    out=w_codes[:, cols].bitcast(FP8X4),
                    scales=w_scales[:, cols],
                    in_=w_grouped[:, n0 * PACK : (n0 + width) * PACK],
                )
            return w_codes, w_scales

        banks = {}

        def project(kind, c, w_codes, w_scales):
            if c == 0 and kind == "v":
                banks[kind] = [
                    psum.tile([P, N], F32, tag="bank", name="v_bank%d" % b) for b in range(B)
                ]
            elif c == 0:
                banks[kind] = [
                    psum.tile([P, ROWS], F32, tag="bank", name="%s_bank%d" % (kind, h))
                    for h in range(H)
                ]
            if kind == "v":
                for b in range(B):
                    x_cols = slice(c * ROWS + b * S, c * ROWS + (b + 1) * S)
                    nc.tensor.matmul_mx(
                        out=banks[kind][b][:],
                        lhsT=x_codes[:, x_cols].bitcast(FP8X4),
                        lhsT_scale=x_scales[:, x_cols],
                        rhs=w_codes[:].bitcast(FP8X4),
                        rhs_scale=w_scales[:],
                        start=(c == 0),
                        stop=(c == PASSES - 1),
                    )
            else:
                x_cols = slice(c * ROWS, (c + 1) * ROWS)
                for h in range(H):
                    w_cols = slice(h * D, (h + 1) * D)
                    nc.tensor.matmul_mx(
                        out=banks[kind][h][:],
                        lhsT=w_codes[:, w_cols].bitcast(FP8X4),
                        lhsT_scale=w_scales[:, w_cols],
                        rhs=x_codes[:, x_cols].bitcast(FP8X4),
                        rhs_scale=x_scales[:, x_cols],
                        start=(c == 0),
                        stop=(c == PASSES - 1),
                    )

        def by_head(t):
            return t[:].rearrange("p (b h i) -> p h b i", b=B, h=H)

        def by_group(t):
            return t[:].rearrange("p (g i) -> p g i", g=GROUPS)

        v_sb = const.tile([P, GROUPS * S], F32)
        score = const.tile([P, GROUPS * S], F32)
        expo = const.tile([P, GROUPS * S], F32)
        weighted = const.tile([P, GROUPS * S], F32)
        summed = const.tile([P, GROUPS * S], F32)
        score_max = const.tile([P, GROUPS], F32)
        exp_bias = const.tile([P, GROUPS], F32)
        exp_sum = const.tile([P, GROUPS], F32)
        inv_sum = const.tile([P, GROUPS], F32)
        weighted_sum = const.tile([P, GROUPS], F32)
        inv_sqrt_d = 1.0 / math.sqrt(D)

        def add_bv():
            for b in range(B):
                nc.vector.tensor_tensor(
                    out=v_sb[:, b * N : (b + 1) * N],
                    in0=banks["v"][b][:],
                    in1=bv_all[:],
                    op=ALU.add,
                )

        def scores():
            for h in range(H):
                nc.vector.scalar_tensor_tensor(
                    out=by_head(score)[:, h],
                    in0=banks["k"][h][:].rearrange("p (b i) -> p b i", b=B),
                    scalar=bk_cols[:, h : h + 1],
                    in1=by_head(v_sb)[:, h],
                    op0=ALU.add,
                    op1=ALU.mult,
                )
            nc.vector.tensor_reduce(
                out=score_max[:], in_=by_group(score), axis=AXIS_X, op=ALU.max
            )
            nc.vector.tensor_scalar_mul(out=exp_bias[:], in0=score_max[:], scalar1=-inv_sqrt_d)

        def exponentials():
            for g in range(GROUPS):
                nc.scalar.activation(
                    out=by_group(expo)[:, g],
                    in_=by_group(score)[:, g],
                    func=ACT.Exp,
                    bias=exp_bias[:, g : g + 1],
                    scale=inv_sqrt_d,
                    accum_out=exp_sum[:, g : g + 1],
                )

        def pool_q():
            for h in range(H):
                nc.vector.scalar_tensor_tensor(
                    out=by_head(weighted)[:, h],
                    in0=banks["q"][h][:].rearrange("p (b i) -> p b i", b=B),
                    scalar=bq_cols[:, h : h + 1],
                    in1=by_head(expo)[:, h],
                    op0=ALU.add,
                    op1=ALU.mult,
                )
                if h < H - 1:
                    for b in range(B):
                        g = b * H + h
                        nc.scalar.activation(
                            out=by_group(summed)[:, g],
                            in_=by_group(weighted)[:, g],
                            func=ACT.Copy,
                            accum_out=weighted_sum[:, g : g + 1],
                        )
            nc.vector.tensor_reduce(
                out=weighted_sum[:, H - 1 :: H],
                in_=by_head(weighted)[:, H - 1],
                axis=AXIS_X,
                op=ALU.add,
            )
            nc.vector.tensor_tensor(
                out=result[:, 0:GROUPS], in0=weighted_sum[:], in1=inv_sum[:], op=ALU.mult
            )
            result_t = psum.tile([P, P], F32, tag="bank")
            nc.tensor.transpose(result_t[:], result[:], ident_f32[:])
            out_rows = const.tile([P, D], F32)
            nc.vector.tensor_copy(out=out_rows[0:GROUPS, :], in_=result_t[0:GROUPS, :])
            nc.sync.dma_start(out=out.rearrange("b h j -> (b h) j"), in_=out_rows[0:GROUPS, :])

        v_done = PASSES + X_LAG
        k_done = 2 * PASSES
        w_ready = {}
        x_banks = {}
        x_ready = {}
        v_ready = {}
        for i in range(len(stream) + 1):
            if i == 1:
                spread_biases()
            x_c = i - X_LAG
            if 0 <= x_c + 1 < PASSES:
                x_banks[x_c + 1] = transpose_x(x_c + 1)
            if i < len(stream):
                w_ready[i] = regroup_w(stream[i][0], stream[i][2], w_raws[i])
                if i + PREFETCH < len(stream):
                    load(i + PREFETCH)
            if 0 <= x_c < PASSES:
                x_ready[x_c] = regroup_x(x_banks[x_c])
            if i >= 1:
                kind, w, c = stream[i - 1]
                w_codes, w_scales = quantise_w(w_ready[i - 1], 2 if i == len(stream) else 1)
                if kind == "v":
                    v_ready[c] = (w_codes, w_scales)
            if 0 <= x_c - 1 < PASSES:
                quantise_x(x_c - 1, x_ready[x_c - 1])
                project("v", x_c - 1, *v_ready[x_c - 1])
            if i >= 1 and kind != "v":
                project(kind, c, w_codes, w_scales)
            if i == v_done + 1:
                add_bv()
            if i == k_done + 1:
                scores()
            if i == k_done + 1 + EXP_LAG:
                exponentials()
            if i == k_done + 1 + 2 * EXP_LAG:
                nc.vector.reciprocal(out=inv_sum[:], in_=exp_sum[:])
        pool_q()
